import numpy as np
import ml_dtypes


def mxq(x, axis, fmt="e4m3"):
    dtype, down = {"e4m3": (ml_dtypes.float8_e4m3fn, 7), "e5m2": (ml_dtypes.float8_e5m2, 14)}[fmt]
    v = np.moveaxis(np.asarray(x, np.float32).astype(ml_dtypes.bfloat16).astype(np.float64), axis, -1)
    blocks = v.reshape(v.shape[:-1] + (-1, 32))
    amax = np.abs(blocks).max(-1, keepdims=True)
    byte = np.maximum(np.where(amax > 0, np.frexp(amax)[1] - 1 + 127, 0) - down, 1)
    scale = np.exp2(byte - 127.0)
    codes = (blocks / scale).astype(np.float32).astype(dtype).astype(np.float64)
    return np.moveaxis((codes * scale).reshape(v.shape), -1, axis)


WIDE = False


def mx_kscale(k):
    if not WIDE:
        return np.ones(k)
    levels = np.array([10, -10, 5, -5, 0])
    if k % 512:
        return np.exp2(np.random.permutation(np.resize(levels, k // 32))).repeat(32)
    a = np.empty((k // 512, 16))
    for p in range(k // 512):
        a[p, :8] = np.random.permutation(np.resize(levels, 8))
        for g in range(8):
            far = levels[np.abs(levels - a[p, g]) >= 10]
            a[p, g + 8] = far[np.random.randint(len(far))]
    return np.exp2(a.ravel()).repeat(32)


BF16 = ml_dtypes.bfloat16


def bf(x):
    return np.asarray(x, np.float32).astype(BF16)


def f64(x):
    return np.asarray(x).astype(np.float64)


B, T, E, H, HKV, DH, WINDOW = 1, 1024, 2048, 8, 4, 128, 512
ROPE_THETA = 10000.0
EPS = 1e-6


def rms_norm(u, w):
    return u * (1.0 / np.sqrt(np.mean(u * u, axis=-1, keepdims=True) + EPS)) * (1.0 + w)


def rotate_half(u):
    return np.concatenate((-u[..., DH // 2:], u[..., :DH // 2]), axis=-1)


def draw0():
    s = mx_kscale(E)
    return {"x": bf(np.random.standard_normal((B, T, E)) * s),
            "wq": bf(np.random.standard_normal((H * DH, E)) / np.sqrt(E) / s),
            "wk": bf(np.random.standard_normal((HKV * DH, E)) / np.sqrt(E) / s),
            "wv": bf(np.random.standard_normal((HKV * DH, E)) * 2.0 / np.sqrt(E) / s),
            "q_norm_w": bf(np.random.standard_normal(DH) * 0.1),
            "k_norm_w": bf(np.random.standard_normal(DH) * 0.1)}


def core(x, wq, wk, wv, q_norm_w, k_norm_w):
    xq = mxq(f64(x), 2, "e4m3")
    q = (xq @ mxq(f64(wq), 1, "e4m3").T).reshape(B, T, H, DH).transpose(0, 2, 1, 3)
    k = (xq @ mxq(f64(wk), 1, "e4m3").T).reshape(B, T, HKV, DH).transpose(0, 2, 1, 3)
    v = (xq @ mxq(f64(wv), 1, "e4m3").T).reshape(B, T, HKV, DH).transpose(0, 2, 1, 3)
    q = rms_norm(q, f64(q_norm_w))
    k = rms_norm(k, f64(k_norm_w))
    pos = f64(np.arange(T))
    inv_freq = 1.0 / (ROPE_THETA ** (f64(np.arange(0, DH, 2)) / DH))
    freqs = pos[:, None] * inv_freq[None, :]
    emb = np.concatenate((freqs, freqs), axis=-1)
    cos = np.cos(emb)[None, None, :, :]
    sin = np.sin(emb)[None, None, :, :]
    q = q * cos + rotate_half(q) * sin
    k = k * cos + rotate_half(k) * sin
    q = q * (DH ** -0.5)
    return q, k, v


def e4m3fn_bytes(y):
    return np.clip(np.asarray(y, np.float64), -448.0, 448.0).astype(np.float32).astype(ml_dtypes.float8_e4m3fn).view(np.uint8)


def e4m3fn_values(b):
    return np.asarray(b, np.uint8).view(ml_dtypes.float8_e4m3fn).astype(np.float64)


def setup_inputs():
    d = draw0()
    x0 = np.asarray(d['x']).astype(np.float64)
    s = (np.max(np.abs(x0), axis=(0, 1), keepdims=True) / 448.0).astype(np.float32)
    out = {}
    for k, v in d.items():
        if k == 'x':
            out['x_bytes'] = e4m3fn_bytes(x0 / s.astype(np.float64))
            out['x_scale'] = s
        else:
            out[k] = v
    return out


def reference(x_bytes, x_scale, wq, wk, wv, q_norm_w, k_norm_w):
    return core(e4m3fn_values(x_bytes) * x_scale.astype(np.float64), wq, wk, wv, q_norm_w, k_norm_w)

@@ -1,0 +1,331 @@
+from contextlib import ExitStack
+import math
+
+import concourse.mybir as mybir
+from concourse.masks import make_identity
+
+TOKENS, FEATURES, HEAD = 1024, 2048, 128
+EPS = 1e-6
+THETA = 10000.0
+FLOPS = 2 * TOKENS * FEATURES * 2048
+
+F32 = mybir.dt.float32
+BF16 = mybir.dt.bfloat16
+U32 = mybir.dt.uint32
+U8 = mybir.dt.uint8
+I32 = mybir.dt.int32
+FP8 = mybir.dt.float8_e4m3fn
+FP8X4 = mybir.dt.float8_e4m3fn_x4
+ALU = mybir.AluOpType
+ACT = mybir.ActivationFunctionType
+
+P = 128
+K_PASS = 512
+PASSES = FEATURES // K_PASS
+TILES = TOKENS // P
+GROUP = 512
+HEADS = GROUP // HEAD
+HALF = HEAD // 2
+WORDS = K_PASS // 2
+
+SQUARES_LAG = 1
+COPY_LAG = 2
+PRODUCTS_LAG = 3
+ADD_LAG = 4
+WIDEN_LEAD = 2
+
+
+def tile_gemma3mhattention_pa_kernel(
+    tc, x_bytes, x_scale, wq, wk, wv, q_norm_w, k_norm_w, out_0, out_1, out_2
+):
+    nc = tc.nc
+    groups = [
+        (wq, 0, out_0, 0, 0),
+        (wq, GROUP, out_0, HEADS, 0),
+        (wk, 0, out_1, 0, 1),
+        (wv, 0, out_2, 0, None),
+    ]
+    n_groups = len(groups)
+
+    later_w = [("w", c, g) for c in range(1, n_groups) for g in range(PASSES)]
+    first_units = [("w", 0, 0), ("w", 0, 1), ("x", 0), ("w", 0, 2), ("w", 0, 3), ("x", 1)]
+    steps = [([unit], None) for unit in first_units]
+    n_mixed = TILES - 2
+    for n in range(n_mixed):
+        steps.append(([later_w[n], ("x", n + 2)], None))
+    for n in range(n_mixed, len(later_w), 2):
+        steps.append((later_w[n : n + 2], None))
+    first_w_only = len(first_units) + n_mixed
+    for i in range(TILES):
+        for c in range(n_groups):
+            steps.append(([], (i, c)))
+    n_steps = len(steps)
+    rope_steps = [t for t in range(n_steps) if steps[t][1] is not None and groups[steps[t][1][1]][4] is not None]
+    n_pairs = len(rope_steps) // 2
+
+    def units_at(t):
+        return steps[t][0] if 0 <= t < n_steps else []
+
+    def bank_at(t):
+        return steps[t][1] if 0 <= t < n_steps else None
+
+    def is_rope(t):
+        return t in rope_steps
+
+    def is_plain(t):
+        return bank_at(t) is not None and not is_rope(t)
+
+    with ExitStack() as ctx:
+        keep = ctx.enter_context(tc.tile_pool(name="keep", bufs=1))
+        work = ctx.enter_context(tc.tile_pool(name="work", bufs=2))
+        ps_t = ctx.enter_context(tc.psum_pool(name="ps_t", bufs=4))
+        ps_a = ctx.enter_context(tc.psum_pool(name="ps_a", bufs=4))
+        ctx.enter_context(tc.manual_schedule())
+
+        scales = keep.tile([P, FEATURES], F32, name="scales")
+        nc.scalar.dma_start(out=scales[:], in_=x_scale.rearrange("a b k -> (a b k)").partition_broadcast(P))
+        norm_w = keep.tile([P, 2, HEAD], BF16, name="norm_w")
+        nc.scalar.dma_start(out=norm_w[:, 0, :], in_=q_norm_w.partition_broadcast(P))
+        nc.scalar.dma_start(out=norm_w[:, 1, :], in_=k_norm_w.partition_broadcast(P))
+
+        x_rows = x_bytes.rearrange("o (i p) k -> p (o i) k", p=P)
+        x_codes_in = keep.tile([P, TILES, FEATURES], U8, name="x_codes_in")
+        w_raw = []
+        for c in range(n_groups):
+            w_raw_c = work.tile([P, HEADS, FEATURES], BF16, name="w_raw%d" % c, tag="big", bufs=4)
+            w_raw.append(w_raw_c)
+
+        def load_w_pass(c, g):
+            w, r0 = groups[c][0], groups[c][1]
+            nc.sync.dma_start(
+                out=w_raw[c][:, :, K_PASS * g : K_PASS * (g + 1)],
+                in_=w[r0 : r0 + GROUP, K_PASS * g : K_PASS * (g + 1)].rearrange("(r p) k -> p r k", p=P),
+            )
+
+        def load_w_heads(c):
+            w, r0 = groups[c][0], groups[c][1]
+            for r in range(HEADS):
+                nc.sync.dma_start(out=w_raw[c][:, r, :], in_=w[r0 + r * P : r0 + (r + 1) * P, :])
+
+        def load_x(i0, i1):
+            nc.sync.dma_start(out=x_codes_in[:, i0:i1, :], in_=x_rows[:, i0:i1, :])
+
+        load_w_pass(0, 0)
+        load_x(0, 1)
+        load_w_pass(0, 1)
+        load_x(1, 2)
+        load_w_pass(0, 2)
+        load_w_pass(0, 3)
+        load_x(2, 4)
+        load_w_pass(1, 0)
+        load_w_pass(1, 1)
+        load_x(4, 6)
+        load_w_pass(1, 2)
+        load_w_pass(1, 3)
+        load_x(6, 8)
+        load_w_heads(2)
+        load_w_heads(3)
+
+        position = keep.tile([P, TILES], F32, name="position")
+        nc.gpsimd.iota(position[:], pattern=[[P, TILES]], base=0, channel_multiplier=1,
+                       allow_small_or_imprecise_dtypes=True)
+        zero = keep.tile([P, 1], F32, name="zero")
+        nc.gpsimd.memset(zero[:], 0.0)
+        warm = keep.tile([P, 1], F32, name="warm")
+        nc.scalar.activation(out=warm[:], in_=zero[:], func=ACT.Sin)
+        ident = keep.tile([P, P], F32, name="ident")
+        make_identity(nc, ident[:])
+
+        coarse = keep.tile([P, TILES, 8], F32, name="coarse")
+        for a in range(8):
+            nc.vector.tensor_scalar_mul(out=coarse[:, :, a], in0=position[:],
+                                        scalar1=THETA ** (-8.0 * a / HALF) / (2.0 * math.pi))
+        turns = keep.tile([P, 2, TILES * 8, 8], F32, name="turns")
+        for b in range(8):
+            nc.vector.tensor_scalar_mul(out=turns[:, 1, :, b], in0=coarse[:].rearrange("p i a -> p (i a)"),
+                                        scalar1=THETA ** (-1.0 * b / HALF))
+        nc.vector.tensor_scalar_add(out=turns[:, 0, :, :], in0=turns[:, 1, :, :], scalar1=0.25)
+        flat = turns[:].rearrange("p c n b -> p (c n b)")
+        whole = keep.tile([P, 2 * TILES * HALF], I32, name="whole")
+        nc.vector.tensor_copy(out=whole[:], in_=flat)
+        nc.vector.scalar_tensor_tensor(out=flat, in0=whole[:], scalar=-1.0, in1=flat, op0=ALU.mult, op1=ALU.add)
+        nc.vector.scalar_tensor_tensor(out=flat, in0=flat, scalar=0.5, in1=flat, op0=ALU.is_gt, op1=ALU.subtract)
+        nc.scalar.activation(out=flat, in_=flat, func=ACT.Sin, scale=-2.0 * math.pi)
+        trig = turns[:].rearrange("p c (i a) b -> p c i (a b)", i=TILES)
+        nc.scalar.activation(out=warm[:], in_=zero[:], func=ACT.Abs_reciprocal_sqrt, bias=1.0)
+
+        gain = keep.tile([P, 2, 2, HEAD], F32, name="gain")
+        tables = []
+        for kind in range(2):
+            table = keep.tile([P, TILES, 2, HEAD], F32, name="table%d" % kind)
+            tables.append(table)
+
+        def build_table(kind):
+            s = HEAD ** -0.5 if kind == 0 else 1.0
+            nc.vector.tensor_scalar(out=gain[:, kind, 0, :], in0=norm_w[:, kind, :],
+                                    scalar1=1.0, scalar2=s, op0=ALU.add, op1=ALU.mult)
+            nc.vector.tensor_scalar(out=gain[:, kind, 1, 0:HALF], in0=norm_w[:, kind, 0:HALF],
+                                    scalar1=1.0, scalar2=s, op0=ALU.add, op1=ALU.mult)
+            nc.vector.tensor_scalar(out=gain[:, kind, 1, HALF:HEAD], in0=norm_w[:, kind, HALF:HEAD],
+                                    scalar1=1.0, scalar2=-s, op0=ALU.add, op1=ALU.mult)
+            for part in range(2):
+                nc.vector.tensor_tensor(
+                    out=tables[kind][:, :, part, :].rearrange("p i (s d) -> p i s d", s=2),
+                    in0=trig[:, part, :, :].unsqueeze(2).to_broadcast([P, TILES, 2, HALF]),
+                    in1=gain[:, kind, part, :].rearrange("p (s d) -> p s d", s=2).unsqueeze(1)
+                    .to_broadcast([P, TILES, 2, HALF]),
+                    op=ALU.mult,
+                )
+
+        x_codes = keep.tile([P, TILES, PASSES * P], U32, name="x_codes", align_bytes=64)
+        x_blocks = keep.tile([P, TILES, PASSES * P], U8, name="x_blocks", align_bytes=64)
+        w_codes, w_blocks = [], []
+        for c in range(n_groups):
+            w_codes_c = keep.tile([P, PASSES, GROUP], U32, name="w_codes%d" % c, align_bytes=64)
+            w_blocks_c = keep.tile([P, PASSES, GROUP], U8, name="w_blocks%d" % c, align_bytes=64)
+            w_codes.append(w_codes_c)
+            w_blocks.append(w_blocks_c)
+
+        x_wide, grouped, turned, sums, squares, inv_rms, products, results = {}, {}, {}, {}, {}, {}, {}, {}
+
+        def widen(i):
+            wide = work.tile([P, FEATURES], BF16, name="wide", tag="wide", bufs=4)
+            nc.vector.tensor_tensor(out=wide[:], in0=x_codes_in[:, i, :].bitcast(FP8), in1=scales[:], op=ALU.mult)
+            x_wide[i] = wide
+
+        def rows_and_pass(unit, n):
+            if unit[0] == "x":
+                return x_wide[unit[1]][:].bitcast(F32), n
+            return w_raw[unit[1]][:, n, :].bitcast(F32), unit[2]
+
+        def transposes(units):
+            for unit in units:
+                group_tile = work.tile([P, 4, P, 4], BF16, name="grouped", tag="grouped", bufs=4, align_bytes=64)
+                grouped[unit] = group_tile
+                banks = []
+                for b in range(2):
+                    bank = ps_t.tile([P, 2, 2, P], F32, name="turned", tag="turned")
+                    banks.append(bank)
+                turned[unit] = banks
+            for unit in units:
+                for a in range(2):
+                    for u in range(2):
+                        for b in range(2):
+                            words, g = rows_and_pass(unit, 2 * b + a)
+                            nc.tensor.transpose(turned[unit][b][:, a, u, :],
+                                                words[:, WORDS * g + u : WORDS * (g + 1) : 2], ident[:])
+
+        def copy_out(unit):
+            words = grouped[unit][:].rearrange("p n r t -> p (n r t)").bitcast(F32)
+            words = words.rearrange("p (n r u) -> p n r u", n=4, u=2)
+            for b in range(2):
+                nc.scalar.copy(out=words[:, 2 * b : 2 * b + 2, :, :],
+                               in_=turned[unit][b][:].rearrange("p a u r -> p a r u"))
+
+        def quantize(unit):
+            values = grouped[unit][:].rearrange("p n r t -> p (n r t)")
+            if unit[0] == "x":
+                codes, blocks = x_codes[:, unit[1], :], x_blocks[:, unit[1], :]
+            else:
+                codes, blocks = w_codes[unit[1]][:, unit[2], :], w_blocks[unit[1]][:, unit[2], :]
+            nc.vector.quantize_mx(out=codes.bitcast(FP8X4), scales=blocks, in_=values)
+
+        def matmuls(t):
+            i, c = bank_at(t)
+            acc = ps_a.tile([P, GROUP], F32, name="acc", tag="acc")
+            for g in range(PASSES):
+                nc.tensor.matmul_mx(
+                    out=acc[:],
+                    lhsT=x_codes[:, i, P * g : P * (g + 1)].bitcast(FP8X4),
+                    lhsT_scale=x_blocks[:, i, P * g : P * (g + 1)],
+                    rhs=w_codes[c][:, g, :].bitcast(FP8X4),
+                    rhs_scale=w_blocks[c][:, g, :],
+                    start=(g == 0),
+                    stop=(g == PASSES - 1),
+                )
+            sums[t] = acc
+
+        def sum_squares(t):
+            total = work.tile([P, HEADS], F32, name="total", tag="total", bufs=6)
+            unused = work.tile([P, HEADS, HEAD], BF16, name="unused", tag="unused", bufs=2)
+            for h in range(HEADS):
+                nc.scalar.activation(out=unused[:, h, :], in_=sums[t][:, HEAD * h : HEAD * (h + 1)], func=ACT.Square,
+                                     accum_out=total[:, h : h + 1])
+            squares[t] = total
+
+        def inverse_rms(t):
+            inv = work.tile([P, HEADS], F32, name="inv", tag="inv", bufs=6)
+            nc.scalar.activation(out=inv[:], in_=squares[t][:], func=ACT.Abs_reciprocal_sqrt, scale=1.0 / HEAD, bias=EPS)
+            inv_rms[t] = inv
+
+        def table_products(t):
+            i, c = bank_at(t)
+            r = rope_steps.index(t)
+            if r % 2 == 0:
+                pair_tile = work.tile([P, 2, 2, HEADS, HEAD], F32, name="pair", tag="big", bufs=4)
+                products[r // 2] = pair_tile
+            for h in range(HEADS):
+                nc.vector.scalar_tensor_tensor(
+                    out=products[r // 2][:, r % 2, :, h, :],
+                    in0=sums[t][:, HEAD * h : HEAD * (h + 1)].unsqueeze(1).to_broadcast([P, 2, HEAD]),
+                    scalar=inv_rms[t][:, h : h + 1],
+                    in1=tables[groups[c][4]][:, i, :, :],
+                    op0=ALU.mult,
+                    op1=ALU.mult,
+                )
+
+        def add_halves(n):
+            result = work.tile([P, 2, HEADS, 2, HALF], F32, name="result", tag="result", bufs=4)
+            parts = products[n][:].rearrange("p b a h (s d) -> p b a h s d", s=2)
+            engine = nc.vector if n == n_pairs - 1 else nc.gpsimd
+            for s in range(2):
+                engine.tensor_tensor(out=result[:, :, :, s, :], in0=parts[:, :, 0, :, s, :],
+                                     in1=parts[:, :, 1, :, 1 - s, :], op=ALU.add)
+            for b in range(2):
+                results[rope_steps[2 * n + b]] = result[:, b, :, :, :]
+
+        def copy_plain(t):
+            plain = work.tile([P, HEADS, 2, HALF], F32, name="plain", tag="plain", bufs=3)
+            nc.vector.tensor_copy(out=plain[:].rearrange("p h s d -> p (h s d)"), in_=sums[t][:])
+            results[t] = plain
+
+        def store(t):
+            i, c = bank_at(t)
+            dst, h0 = groups[c][2], groups[c][3]
+            nc.sync.dma_start(
+                out=dst[0, h0 : h0 + HEADS, P * i : P * (i + 1), :].rearrange("h p d -> p h d"),
+                in_=results[t][:].rearrange("p h s d -> p h (s d)"),
+            )
+
+        for unit in first_units:
+            if unit[0] == "x":
+                widen(unit[1])
+        for t in range(n_steps + ADD_LAG + 1):
+            if units_at(t):
+                transposes(units_at(t))
+            if bank_at(t) is not None:
+                matmuls(t)
+            if is_rope(t - SQUARES_LAG):
+                sum_squares(t - SQUARES_LAG)
+                inverse_rms(t - SQUARES_LAG)
+            for unit in units_at(t):
+                copy_out(unit)
+            if is_rope(t - PRODUCTS_LAG):
+                table_products(t - PRODUCTS_LAG)
+            if is_plain(t - COPY_LAG):
+                copy_plain(t - COPY_LAG)
+                store(t - COPY_LAG)
+            for unit in units_at(t - 1):
+                quantize(unit)
+            for unit in units_at(t + WIDEN_LEAD):
+                if unit[0] == "x" and unit[1] not in x_wide:
+                    widen(unit[1])
+            if t == first_w_only:
+                build_table(0)
+            if t == first_w_only + 1:
+                build_table(1)
+            if is_rope(t - ADD_LAG) and rope_steps.index(t - ADD_LAG) % 2 == 1:
+                pair = rope_steps.index(t - ADD_LAG) // 2
+                add_halves(pair)
+                store(rope_steps[2 * pair])
+                store(rope_steps[2 * pair + 1])

@@ -144,13 +144,16 @@ def tile_gemma3mhattention_pa_kernel(
         for b in range(8):
             nc.vector.tensor_scalar_mul(out=turns[:, 1, :, b], in0=coarse[:].rearrange("p i a -> p (i a)"),
                                         scalar1=THETA ** (-1.0 * b / HALF))
-        nc.vector.tensor_scalar_add(out=turns[:, 0, :, :], in0=turns[:, 1, :, :], scalar1=0.25)
-        flat = turns[:].rearrange("p c n b -> p (c n b)")
-        whole = keep.tile([P, 2 * TILES * HALF], I32, name="whole")
-        nc.vector.tensor_copy(out=whole[:], in_=flat)
-        nc.vector.scalar_tensor_tensor(out=flat, in0=whole[:], scalar=-1.0, in1=flat, op0=ALU.mult, op1=ALU.add)
-        nc.vector.scalar_tensor_tensor(out=flat, in0=flat, scalar=0.5, in1=flat, op0=ALU.is_gt, op1=ALU.subtract)
-        nc.scalar.activation(out=flat, in_=flat, func=ACT.Sin, scale=-2.0 * math.pi)
+        for_cos = turns[:, 0, :, :].rearrange("p n b -> p (n b)")
+        for_sin = turns[:, 1, :, :].rearrange("p n b -> p (n b)")
+        whole = keep.tile([P, TILES * HALF], I32, name="whole")
+        nc.vector.tensor_copy(out=whole[:], in_=for_sin)
+        nc.vector.scalar_tensor_tensor(out=for_sin, in0=whole[:], scalar=-1.0, in1=for_sin, op0=ALU.mult, op1=ALU.add)
+        nc.vector.scalar_tensor_tensor(out=for_sin, in0=for_sin, scalar=0.5, in1=for_sin, op0=ALU.is_gt, op1=ALU.subtract)
+        nc.scalar.activation(out=for_cos, in_=for_sin, func=ACT.Abs)
+        nc.scalar.activation(out=for_cos, in_=for_cos, func=ACT.Copy, scale=-1.0, bias=0.25)
+        nc.scalar.activation(out=for_cos, in_=for_cos, func=ACT.Sin, scale=2.0 * math.pi)
+        nc.scalar.activation(out=for_sin, in_=for_sin, func=ACT.Sin, scale=-2.0 * math.pi)
         trig = turns[:].rearrange("p c (i a) b -> p c i (a b)", i=TILES)
         nc.scalar.activation(out=warm[:], in_=zero[:], func=ACT.Abs_reciprocal_sqrt, bias=1.0)
 
@@ -286,7 +289,7 @@ def tile_gemma3mhattention_pa_kernel(
 
         def copy_plain(t):
             plain = work.tile([P, HEADS, 2, HALF], F32, name="plain", tag="plain", bufs=3)
-            nc.vector.tensor_copy(out=plain[:].rearrange("p h s d -> p (h s d)"), in_=sums[t][:])
+            nc.scalar.copy(out=plain[:].rearrange("p h s d -> p (h s d)"), in_=sums[t][:])
             results[t] = plain
 
         def store(t):
@@ -308,13 +311,13 @@ def tile_gemma3mhattention_pa_kernel(
             if is_rope(t - SQUARES_LAG):
                 sum_squares(t - SQUARES_LAG)
                 inverse_rms(t - SQUARES_LAG)
+            if is_plain(t - COPY_LAG):
+                copy_plain(t - COPY_LAG)
+                store(t - COPY_LAG)
             for unit in units_at(t):
                 copy_out(unit)
             if is_rope(t - PRODUCTS_LAG):
                 table_products(t - PRODUCTS_LAG)
-            if is_plain(t - COPY_LAG):
-                copy_plain(t - COPY_LAG)
-                store(t - COPY_LAG)
             for unit in units_at(t - 1):
                 quantize(unit)
             for unit in units_at(t + WIDEN_LEAD):

@@ -32,7 +32,9 @@ SQUARES_LAG = 1
 COPY_LAG = 2
 PRODUCTS_LAG = 3
 ADD_LAG = 4
-WIDEN_LEAD = 2
+WIDEN_LEAD = 3
+LOAD_LEAD = 3
+V_LAST = 2
 
 
 def tile_gemma3mhattention_pa_kernel(
@@ -47,18 +49,17 @@ def tile_gemma3mhattention_pa_kernel(
     ]
     n_groups = len(groups)
 
-    later_w = [("w", c, g) for c in range(1, n_groups) for g in range(PASSES)]
-    first_units = [("w", 0, 0), ("w", 0, 1), ("x", 0), ("w", 0, 2), ("w", 0, 3), ("x", 1)]
-    steps = [([unit], None) for unit in first_units]
-    n_mixed = TILES - 2
-    for n in range(n_mixed):
-        steps.append(([later_w[n], ("x", n + 2)], None))
-    for n in range(n_mixed, len(later_w), 2):
-        steps.append((later_w[n : n + 2], None))
-    first_w_only = len(first_units) + n_mixed
+    steps = [([("w", 0, 0)], None)]
+    for n in range(TILES):
+        for m in range(2 * n + 1, min(2 * n + 3, n_groups * PASSES)):
+            steps.append(([("w", m // PASSES, m % PASSES)], None))
+        steps.append(([("x", n)], None))
     for i in range(TILES):
         for c in range(n_groups):
-            steps.append(([], (i, c)))
+            if groups[c][4] is not None or i < TILES - V_LAST:
+                steps.append(([], (i, c)))
+    for i in range(TILES - V_LAST, TILES):
+        steps.append(([], (i, n_groups - 1)))
     n_steps = len(steps)
     rope_steps = [t for t in range(n_steps) if steps[t][1] is not None and groups[steps[t][1][1]][4] is not None]
     n_pairs = len(rope_steps) // 2
@@ -78,8 +79,7 @@ def tile_gemma3mhattention_pa_kernel(
     with ExitStack() as ctx:
         keep = ctx.enter_context(tc.tile_pool(name="keep", bufs=1))
         work = ctx.enter_context(tc.tile_pool(name="work", bufs=2))
-        ps_t = ctx.enter_context(tc.psum_pool(name="ps_t", bufs=4))
-        ps_a = ctx.enter_context(tc.psum_pool(name="ps_a", bufs=4))
+        ps = ctx.enter_context(tc.psum_pool(name="ps", bufs=8))
         ctx.enter_context(tc.manual_schedule())
 
         scales = keep.tile([P, FEATURES], F32, name="scales")
@@ -92,39 +92,26 @@ def tile_gemma3mhattention_pa_kernel(
         x_codes_in = keep.tile([P, TILES, FEATURES], U8, name="x_codes_in")
         w_raw = []
         for c in range(n_groups):
-            w_raw_c = work.tile([P, HEADS, FEATURES], BF16, name="w_raw%d" % c, tag="big", bufs=4)
+            w_raw_c = work.tile([P, PASSES, HEADS, K_PASS], BF16, name="w_raw%d" % c, tag="big", bufs=4)
             w_raw.append(w_raw_c)
 
         def load_w_pass(c, g):
             w, r0 = groups[c][0], groups[c][1]
             nc.sync.dma_start(
-                out=w_raw[c][:, :, K_PASS * g : K_PASS * (g + 1)],
+                out=w_raw[c][:, g, :, :],
                 in_=w[r0 : r0 + GROUP, K_PASS * g : K_PASS * (g + 1)].rearrange("(r p) k -> p r k", p=P),
             )
-
-        def load_w_heads(c):
-            w, r0 = groups[c][0], groups[c][1]
-            for r in range(HEADS):
-                nc.sync.dma_start(out=w_raw[c][:, r, :], in_=w[r0 + r * P : r0 + (r + 1) * P, :])
 
         def load_x(i0, i1):
             nc.sync.dma_start(out=x_codes_in[:, i0:i1, :], in_=x_rows[:, i0:i1, :])
 
-        load_w_pass(0, 0)
-        load_x(0, 1)
-        load_w_pass(0, 1)
-        load_x(1, 2)
-        load_w_pass(0, 2)
-        load_w_pass(0, 3)
-        load_x(2, 4)
-        load_w_pass(1, 0)
-        load_w_pass(1, 1)
-        load_x(4, 6)
-        load_w_pass(1, 2)
-        load_w_pass(1, 3)
-        load_x(6, 8)
-        load_w_heads(2)
-        load_w_heads(3)
+        for t in range(n_steps):
+            for unit in units_at(t):
+                if unit[0] == "w":
+                    load_w_pass(unit[1], unit[2])
+            for unit in units_at(t + LOAD_LEAD):
+                if unit[0] == "x":
+                    load_x(unit[1], unit[1] + 1)
 
         position = keep.tile([P, TILES], F32, name="position")
         nc.gpsimd.iota(position[:], pattern=[[P, TILES]], base=0, channel_multiplier=1,
@@ -155,7 +142,6 @@ def tile_gemma3mhattention_pa_kernel(
         nc.scalar.activation(out=for_cos, in_=for_cos, func=ACT.Sin, scale=2.0 * math.pi)
         nc.scalar.activation(out=for_sin, in_=for_sin, func=ACT.Sin, scale=-2.0 * math.pi)
         trig = turns[:].rearrange("p c (i a) b -> p c i (a b)", i=TILES)
-        nc.scalar.activation(out=warm[:], in_=zero[:], func=ACT.Abs_reciprocal_sqrt, bias=1.0)
 
         gain = keep.tile([P, 2, 2, HEAD], F32, name="gain")
         tables = []
@@ -189,6 +175,7 @@ def tile_gemma3mhattention_pa_kernel(
             w_codes.append(w_codes_c)
             w_blocks.append(w_blocks_c)
 
+        built = []
         x_wide, grouped, turned, sums, squares, inv_rms, products, results = {}, {}, {}, {}, {}, {}, {}, {}
 
         def widen(i):
@@ -198,8 +185,8 @@ def tile_gemma3mhattention_pa_kernel(
 
         def rows_and_pass(unit, n):
             if unit[0] == "x":
-                return x_wide[unit[1]][:].bitcast(F32), n
-            return w_raw[unit[1]][:, n, :].bitcast(F32), unit[2]
+                return x_wide[unit[1]][:, K_PASS * n : K_PASS * (n + 1)].bitcast(F32)
+            return w_raw[unit[1]][:, unit[2], n, :].bitcast(F32)
 
         def transposes(units):
             for unit in units:
@@ -207,16 +194,15 @@ def tile_gemma3mhattention_pa_kernel(
                 grouped[unit] = group_tile
                 banks = []
                 for b in range(2):
-                    bank = ps_t.tile([P, 2, 2, P], F32, name="turned", tag="turned")
+                    bank = ps.tile([P, 2, 2, P], F32, name="turned", tag="bank")
                     banks.append(bank)
                 turned[unit] = banks
             for unit in units:
                 for a in range(2):
                     for u in range(2):
                         for b in range(2):
-                            words, g = rows_and_pass(unit, 2 * b + a)
-                            nc.tensor.transpose(turned[unit][b][:, a, u, :],
-                                                words[:, WORDS * g + u : WORDS * (g + 1) : 2], ident[:])
+                            words = rows_and_pass(unit, 2 * b + a)
+                            nc.tensor.transpose(turned[unit][b][:, a, u, :], words[:, u : WORDS : 2], ident[:])
 
         def copy_out(unit):
             words = grouped[unit][:].rearrange("p n r t -> p (n r t)").bitcast(F32)
@@ -235,7 +221,7 @@ def tile_gemma3mhattention_pa_kernel(
 
         def matmuls(t):
             i, c = bank_at(t)
-            acc = ps_a.tile([P, GROUP], F32, name="acc", tag="acc")
+            acc = ps.tile([P, GROUP], F32, name="acc", tag="bank")
             for g in range(PASSES):
                 nc.tensor.matmul_mx(
                     out=acc[:],
@@ -264,6 +250,9 @@ def tile_gemma3mhattention_pa_kernel(
         def table_products(t):
             i, c = bank_at(t)
             r = rope_steps.index(t)
+            if groups[c][4] not in built:
+                build_table(groups[c][4])
+                built.append(groups[c][4])
             if r % 2 == 0:
                 pair_tile = work.tile([P, 2, 2, HEADS, HEAD], F32, name="pair", tag="big", bufs=4)
                 products[r // 2] = pair_tile
@@ -300,9 +289,10 @@ def tile_gemma3mhattention_pa_kernel(
                 in_=results[t][:].rearrange("p h s d -> p h (s d)"),
             )
 
-        for unit in first_units:
-            if unit[0] == "x":
-                widen(unit[1])
+        for t in range(WIDEN_LEAD):
+            for unit in units_at(t):
+                if unit[0] == "x":
+                    widen(unit[1])
         for t in range(n_steps + ADD_LAG + 1):
             if units_at(t):
                 transposes(units_at(t))
@@ -316,6 +306,8 @@ def tile_gemma3mhattention_pa_kernel(
                 store(t - COPY_LAG)
             for unit in units_at(t):
                 copy_out(unit)
+            if units_at(t) and not units_at(t + 1):
+                nc.scalar.activation(out=warm[:], in_=zero[:], func=ACT.Abs_reciprocal_sqrt, bias=1.0)
             if is_rope(t - PRODUCTS_LAG):
                 table_products(t - PRODUCTS_LAG)
             for unit in units_at(t - 1):
@@ -323,10 +315,6 @@ def tile_gemma3mhattention_pa_kernel(
             for unit in units_at(t + WIDEN_LEAD):
                 if unit[0] == "x" and unit[1] not in x_wide:
                     widen(unit[1])
-            if t == first_w_only:
-                build_table(0)
-            if t == first_w_only + 1:
-                build_table(1)
             if is_rope(t - ADD_LAG) and rope_steps.index(t - ADD_LAG) % 2 == 1:
                 pair = rope_steps.index(t - ADD_LAG) // 2
                 add_halves(pair)

@@ -32,8 +32,8 @@ SQUARES_LAG = 1
 COPY_LAG = 2
 PRODUCTS_LAG = 3
 ADD_LAG = 4
-WIDEN_LEAD = 3
-LOAD_LEAD = 3
+WIDEN_LEAD = 5
+LOAD_LEAD = 6
 V_LAST = 2
 
 
@@ -83,7 +83,7 @@ def tile_gemma3mhattention_pa_kernel(
         ctx.enter_context(tc.manual_schedule())
 
         scales = keep.tile([P, FEATURES], F32, name="scales")
-        nc.scalar.dma_start(out=scales[:], in_=x_scale.rearrange("a b k -> (a b k)").partition_broadcast(P))
+        nc.sync.dma_start(out=scales[:], in_=x_scale.rearrange("a b k -> (a b k)").partition_broadcast(P))
         norm_w = keep.tile([P, 2, HEAD], BF16, name="norm_w")
         nc.scalar.dma_start(out=norm_w[:, 0, :], in_=q_norm_w.partition_broadcast(P))
         nc.scalar.dma_start(out=norm_w[:, 1, :], in_=k_norm_w.partition_broadcast(P))
@@ -105,7 +105,7 @@ def tile_gemma3mhattention_pa_kernel(
         def load_x(i0, i1):
             nc.sync.dma_start(out=x_codes_in[:, i0:i1, :], in_=x_rows[:, i0:i1, :])
 
-        for t in range(n_steps):
+        for t in range(-LOAD_LEAD, n_steps):
             for unit in units_at(t):
                 if unit[0] == "w":
                     load_w_pass(unit[1], unit[2])
@@ -123,25 +123,27 @@ def tile_gemma3mhattention_pa_kernel(
         ident = keep.tile([P, P], F32, name="ident")
         make_identity(nc, ident[:])
 
-        coarse = keep.tile([P, TILES, 8], F32, name="coarse")
+        coarse = keep.tile([P, 8, TILES], F32, name="coarse")
         for a in range(8):
-            nc.vector.tensor_scalar_mul(out=coarse[:, :, a], in0=position[:],
+            nc.vector.tensor_scalar_mul(out=coarse[:, a, :], in0=position[:],
                                         scalar1=THETA ** (-8.0 * a / HALF) / (2.0 * math.pi))
-        turns = keep.tile([P, 2, TILES * 8, 8], F32, name="turns")
+        angles = keep.tile([P, 2, 8, 8 * TILES], F32, name="angles")
         for b in range(8):
-            nc.vector.tensor_scalar_mul(out=turns[:, 1, :, b], in0=coarse[:].rearrange("p i a -> p (i a)"),
+            nc.vector.tensor_scalar_mul(out=angles[:, 1, b, :], in0=coarse[:].rearrange("p a i -> p (a i)"),
                                         scalar1=THETA ** (-1.0 * b / HALF))
-        for_cos = turns[:, 0, :, :].rearrange("p n b -> p (n b)")
-        for_sin = turns[:, 1, :, :].rearrange("p n b -> p (n b)")
+        for_cos = angles[:, 0, :, :].rearrange("p b n -> p (b n)")
+        for_sin = angles[:, 1, :, :].rearrange("p b n -> p (b n)")
         whole = keep.tile([P, TILES * HALF], I32, name="whole")
         nc.vector.tensor_copy(out=whole[:], in_=for_sin)
         nc.vector.scalar_tensor_tensor(out=for_sin, in0=whole[:], scalar=-1.0, in1=for_sin, op0=ALU.mult, op1=ALU.add)
         nc.vector.scalar_tensor_tensor(out=for_sin, in0=for_sin, scalar=0.5, in1=for_sin, op0=ALU.is_gt, op1=ALU.subtract)
         nc.scalar.activation(out=for_cos, in_=for_sin, func=ACT.Abs)
         nc.scalar.activation(out=for_cos, in_=for_cos, func=ACT.Copy, scale=-1.0, bias=0.25)
-        nc.scalar.activation(out=for_cos, in_=for_cos, func=ACT.Sin, scale=2.0 * math.pi)
-        nc.scalar.activation(out=for_sin, in_=for_sin, func=ACT.Sin, scale=-2.0 * math.pi)
-        trig = turns[:].rearrange("p c (i a) b -> p c i (a b)", i=TILES)
+        trig = keep.tile([P, 2, TILES, HALF], F32, name="trig")
+        for part, turn in ((0, 2.0 * math.pi), (1, -2.0 * math.pi)):
+            nc.scalar.activation(out=trig[:, part, :, :].rearrange("p i (a b) -> p i a b", b=8),
+                                 in_=angles[:, part, :, :].rearrange("p b (a i) -> p i a b", i=TILES),
+                                 func=ACT.Sin, scale=turn)
 
         gain = keep.tile([P, 2, 2, HEAD], F32, name="gain")
         tables = []
@@ -149,7 +151,7 @@ def tile_gemma3mhattention_pa_kernel(
             table = keep.tile([P, TILES, 2, HEAD], F32, name="table%d" % kind)
             tables.append(table)
 
-        def build_table(kind):
+        def build_gain(kind):
             s = HEAD ** -0.5 if kind == 0 else 1.0
             nc.vector.tensor_scalar(out=gain[:, kind, 0, :], in0=norm_w[:, kind, :],
                                     scalar1=1.0, scalar2=s, op0=ALU.add, op1=ALU.mult)
@@ -157,6 +159,11 @@ def tile_gemma3mhattention_pa_kernel(
                                     scalar1=1.0, scalar2=s, op0=ALU.add, op1=ALU.mult)
             nc.vector.tensor_scalar(out=gain[:, kind, 1, HALF:HEAD], in0=norm_w[:, kind, HALF:HEAD],
                                     scalar1=1.0, scalar2=-s, op0=ALU.add, op1=ALU.mult)
+
+        build_gain(0)
+        build_gain(1)
+
+        def build_table(kind):
             for part in range(2):
                 nc.vector.tensor_tensor(
                     out=tables[kind][:, :, part, :].rearrange("p i (s d) -> p i s d", s=2),
@@ -269,7 +276,7 @@ def tile_gemma3mhattention_pa_kernel(
         def add_halves(n):
             result = work.tile([P, 2, HEADS, 2, HALF], F32, name="result", tag="result", bufs=4)
             parts = products[n][:].rearrange("p b a h (s d) -> p b a h s d", s=2)
-            engine = nc.vector if n == n_pairs - 1 else nc.gpsimd
+            engine = nc.vector if n >= n_pairs - 2 else nc.gpsimd
             for s in range(2):
                 engine.tensor_tensor(out=result[:, :, :, s, :], in0=parts[:, :, 0, :, s, :],
                                      in1=parts[:, :, 1, :, 1 - s, :], op=ALU.add)
@@ -310,11 +317,11 @@ def tile_gemma3mhattention_pa_kernel(
                 nc.scalar.activation(out=warm[:], in_=zero[:], func=ACT.Abs_reciprocal_sqrt, bias=1.0)
             if is_rope(t - PRODUCTS_LAG):
                 table_products(t - PRODUCTS_LAG)
-            for unit in units_at(t - 1):
-                quantize(unit)
             for unit in units_at(t + WIDEN_LEAD):
                 if unit[0] == "x" and unit[1] not in x_wide:
                     widen(unit[1])
+            for unit in units_at(t - 1):
+                quantize(unit)
             if is_rope(t - ADD_LAG) and rope_steps.index(t - ADD_LAG) % 2 == 1:
                 pair = rope_steps.index(t - ADD_LAG) // 2
                 add_halves(pair)

@@ -145,31 +145,33 @@ def tile_gemma3mhattention_pa_kernel(
                                  in_=angles[:, part, :, :].rearrange("p b (a i) -> p i a b", i=TILES),
                                  func=ACT.Sin, scale=turn)
 
-        gain = keep.tile([P, 2, 2, HEAD], F32, name="gain")
+        gain = keep.tile([P, 2, 3, HALF], F32, name="gain")
         tables = []
         for kind in range(2):
-            table = keep.tile([P, TILES, 2, HEAD], F32, name="table%d" % kind)
+            table = keep.tile([P, TILES, 2, 2, HALF], F32, name="table%d" % kind)
             tables.append(table)
 
         def build_gain(kind):
             s = HEAD ** -0.5 if kind == 0 else 1.0
-            nc.vector.tensor_scalar(out=gain[:, kind, 0, :], in0=norm_w[:, kind, :],
-                                    scalar1=1.0, scalar2=s, op0=ALU.add, op1=ALU.mult)
-            nc.vector.tensor_scalar(out=gain[:, kind, 1, 0:HALF], in0=norm_w[:, kind, 0:HALF],
-                                    scalar1=1.0, scalar2=s, op0=ALU.add, op1=ALU.mult)
-            nc.vector.tensor_scalar(out=gain[:, kind, 1, HALF:HEAD], in0=norm_w[:, kind, HALF:HEAD],
-                                    scalar1=1.0, scalar2=-s, op0=ALU.add, op1=ALU.mult)
+            for n, (half, factor) in enumerate(((0, s), (1, -s), (1, s))):
+                nc.vector.tensor_scalar(out=gain[:, kind, n, :], in0=norm_w[:, kind, HALF * half : HALF * (half + 1)],
+                                        scalar1=1.0, scalar2=factor, op0=ALU.add, op1=ALU.mult)
 
         build_gain(0)
         build_gain(1)
 
         def build_table(kind):
-            for part in range(2):
+            nc.vector.tensor_tensor(
+                out=tables[kind][:, :, :, 0, :],
+                in0=trig[:].rearrange("p c i d -> p i c d"),
+                in1=gain[:, kind, 0, :].unsqueeze(1).unsqueeze(1).to_broadcast([P, TILES, 2, HALF]),
+                op=ALU.mult,
+            )
+            for dst in range(2):
                 nc.vector.tensor_tensor(
-                    out=tables[kind][:, :, part, :].rearrange("p i (s d) -> p i s d", s=2),
-                    in0=trig[:, part, :, :].unsqueeze(2).to_broadcast([P, TILES, 2, HALF]),
-                    in1=gain[:, kind, part, :].rearrange("p (s d) -> p s d", s=2).unsqueeze(1)
-                    .to_broadcast([P, TILES, 2, HALF]),
+                    out=tables[kind][:, :, dst, 1, :],
+                    in0=trig[:, 1 - dst, :, :],
+                    in1=gain[:, kind, 1 + dst, :].unsqueeze(1).to_broadcast([P, TILES, HALF]),
                     op=ALU.mult,
                 )
 
@@ -261,31 +263,30 @@ def tile_gemma3mhattention_pa_kernel(
                 build_table(groups[c][4])
                 built.append(groups[c][4])
             if r % 2 == 0:
-                pair_tile = work.tile([P, 2, 2, HEADS, HEAD], F32, name="pair", tag="big", bufs=4)
+                pair_tile = work.tile([P, 2, HEADS, 2, 2, HALF], F32, name="pair", tag="big", bufs=4)
                 products[r // 2] = pair_tile
             for h in range(HEADS):
                 nc.vector.scalar_tensor_tensor(
-                    out=products[r // 2][:, r % 2, :, h, :],
+                    out=products[r // 2][:, r % 2, h, :, :, :].rearrange("p t s d -> p t (s d)"),
                     in0=sums[t][:, HEAD * h : HEAD * (h + 1)].unsqueeze(1).to_broadcast([P, 2, HEAD]),
                     scalar=inv_rms[t][:, h : h + 1],
-                    in1=tables[groups[c][4]][:, i, :, :],
+                    in1=tables[groups[c][4]][:, i, :, :, :].rearrange("p t s d -> p t (s d)"),
                     op0=ALU.mult,
                     op1=ALU.mult,
                 )
 
         def add_halves(n):
-            result = work.tile([P, 2, HEADS, 2, HALF], F32, name="result", tag="result", bufs=4)
-            parts = products[n][:].rearrange("p b a h (s d) -> p b a h s d", s=2)
+            result = work.tile([P, 2, HEADS, HEAD], F32, name="result", tag="result", bufs=4)
+            shares = products[n][:].rearrange("p b h t s d -> p (b h t) s d")
             engine = nc.vector if n >= n_pairs - 2 else nc.gpsimd
-            for s in range(2):
-                engine.tensor_tensor(out=result[:, :, :, s, :], in0=parts[:, :, 0, :, s, :],
-                                     in1=parts[:, :, 1, :, 1 - s, :], op=ALU.add)
+            engine.tensor_tensor(out=result[:].rearrange("p b h (t d) -> p (b h t) d", t=2), in0=shares[:, :, 0, :],
+                                 in1=shares[:, :, 1, :], op=ALU.add)
             for b in range(2):
-                results[rope_steps[2 * n + b]] = result[:, b, :, :, :]
+                results[rope_steps[2 * n + b]] = result[:, b, :, :]
 
         def copy_plain(t):
-            plain = work.tile([P, HEADS, 2, HALF], F32, name="plain", tag="plain", bufs=3)
-            nc.scalar.copy(out=plain[:].rearrange("p h s d -> p (h s d)"), in_=sums[t][:])
+            plain = work.tile([P, HEADS, HEAD], F32, name="plain", tag="plain", bufs=3)
+            nc.scalar.copy(out=plain[:].rearrange("p h e -> p (h e)"), in_=sums[t][:])
             results[t] = plain
 
         def store(t):
@@ -293,7 +294,7 @@ def tile_gemma3mhattention_pa_kernel(
             dst, h0 = groups[c][2], groups[c][3]
             nc.sync.dma_start(
                 out=dst[0, h0 : h0 + HEADS, P * i : P * (i + 1), :].rearrange("h p d -> p h d"),
-                in_=results[t][:].rearrange("p h s d -> p h (s d)"),
+                in_=results[t][:],
             )
 
         for t in range(WIDEN_LEAD):

@@ -175,12 +175,12 @@ def tile_gemma3mhattention_pa_kernel(
                     op=ALU.mult,
                 )
 
-        x_codes = keep.tile([P, TILES, PASSES * P], U32, name="x_codes", align_bytes=64)
-        x_blocks = keep.tile([P, TILES, PASSES * P], U8, name="x_blocks", align_bytes=64)
+        x_codes = keep.tile([P, TILES, PASSES * P], U32, name="x_codes", align_bytes=256)
+        x_blocks = keep.tile([P, TILES, PASSES * P], U8, name="x_blocks", align_bytes=256)
         w_codes, w_blocks = [], []
         for c in range(n_groups):
-            w_codes_c = keep.tile([P, PASSES, GROUP], U32, name="w_codes%d" % c, align_bytes=64)
-            w_blocks_c = keep.tile([P, PASSES, GROUP], U8, name="w_blocks%d" % c, align_bytes=64)
+            w_codes_c = keep.tile([P, PASSES, GROUP], U32, name="w_codes%d" % c, align_bytes=256)
+            w_blocks_c = keep.tile([P, PASSES, GROUP], U8, name="w_blocks%d" % c, align_bytes=256)
             w_codes.append(w_codes_c)
             w_blocks.append(w_blocks_c)
 

@@ -82,8 +82,9 @@ def tile_gemma3mhattention_pa_kernel(
         ps = ctx.enter_context(tc.psum_pool(name="ps", bufs=8))
         ctx.enter_context(tc.manual_schedule())
 
+        scale_cols = keep.tile([P, PASSES, 4], F32, name="scale_cols")
+        nc.sync.dma_start(out=scale_cols[:], in_=x_scale.rearrange("a b (g q t) -> (a b q) g t", g=PASSES, t=4))
         scales = keep.tile([P, FEATURES], F32, name="scales")
-        nc.sync.dma_start(out=scales[:], in_=x_scale.rearrange("a b k -> (a b k)").partition_broadcast(P))
         norm_w = keep.tile([P, 2, HEAD], BF16, name="norm_w")
         nc.scalar.dma_start(out=norm_w[:, 0, :], in_=q_norm_w.partition_broadcast(P))
         nc.scalar.dma_start(out=norm_w[:, 1, :], in_=k_norm_w.partition_broadcast(P))
@@ -122,6 +123,13 @@ def tile_gemma3mhattention_pa_kernel(
         nc.scalar.activation(out=warm[:], in_=zero[:], func=ACT.Sin)
         ident = keep.tile([P, P], F32, name="ident")
         make_identity(nc, ident[:])
+
+        for g in range(PASSES):
+            spread = ps.tile([P, 4, P], F32, name="spread", tag="bank")
+            for n in range(4):
+                nc.tensor.transpose(spread[:, n, :], scale_cols[:, g, n : n + 1].to_broadcast([P, P]), ident[:])
+            nc.scalar.copy(out=scales[:, K_PASS * g : K_PASS * (g + 1)].rearrange("p (q t) -> p q t", t=4),
+                           in_=spread[:].rearrange("p t q -> p q t"))
 
         coarse = keep.tile([P, 8, TILES], F32, name="coarse")
         for a in range(8):
@@ -189,7 +197,10 @@ def tile_gemma3mhattention_pa_kernel(
 
         def widen(i):
             wide = work.tile([P, FEATURES], BF16, name="wide", tag="wide", bufs=4)
-            nc.vector.tensor_tensor(out=wide[:], in0=x_codes_in[:, i, :].bitcast(FP8), in1=scales[:], op=ALU.mult)
+            width = K_PASS if i == 0 else FEATURES
+            for k0 in range(0, FEATURES, width):
+                nc.vector.tensor_tensor(out=wide[:, k0 : k0 + width], in0=x_codes_in[:, i, k0 : k0 + width].bitcast(FP8),
+                                        in1=scales[:, k0 : k0 + width], op=ALU.mult)
             x_wide[i] = wide
 
         def rows_and_pass(unit, n):

@@ -34,6 +34,7 @@ PRODUCTS_LAG = 3
 ADD_LAG = 4
 WIDEN_LEAD = 5
 LOAD_LEAD = 6
+SINES_STEP = 12
 V_LAST = 2
 
 
@@ -49,9 +50,9 @@ def tile_gemma3mhattention_pa_kernel(
     ]
     n_groups = len(groups)
 
-    steps = [([("w", 0, 0)], None)]
+    steps = []
     for n in range(TILES):
-        for m in range(2 * n + 1, min(2 * n + 3, n_groups * PASSES)):
+        for m in (2 * n, 2 * n + 1):
             steps.append(([("w", m // PASSES, m % PASSES)], None))
         steps.append(([("x", n)], None))
     for i in range(TILES):
@@ -86,8 +87,6 @@ def tile_gemma3mhattention_pa_kernel(
         nc.sync.dma_start(out=scale_cols[:], in_=x_scale.rearrange("a b (g q t) -> (a b q) g t", g=PASSES, t=4))
         scales = keep.tile([P, FEATURES], F32, name="scales")
         norm_w = keep.tile([P, 2, HEAD], BF16, name="norm_w")
-        nc.scalar.dma_start(out=norm_w[:, 0, :], in_=q_norm_w.partition_broadcast(P))
-        nc.scalar.dma_start(out=norm_w[:, 1, :], in_=k_norm_w.partition_broadcast(P))
 
         x_rows = x_bytes.rearrange("o (i p) k -> p (o i) k", p=P)
         x_codes_in = keep.tile([P, TILES, FEATURES], U8, name="x_codes_in")
@@ -113,6 +112,8 @@ def tile_gemma3mhattention_pa_kernel(
             for unit in units_at(t + LOAD_LEAD):
                 if unit[0] == "x":
                     load_x(unit[1], unit[1] + 1)
+        nc.sync.dma_start(out=norm_w[:, 0, :], in_=q_norm_w.partition_broadcast(P))
+        nc.sync.dma_start(out=norm_w[:, 1, :], in_=k_norm_w.partition_broadcast(P))
 
         position = keep.tile([P, TILES], F32, name="position")
         nc.gpsimd.iota(position[:], pattern=[[P, TILES]], base=0, channel_multiplier=1,
@@ -145,13 +146,15 @@ def tile_gemma3mhattention_pa_kernel(
         nc.vector.tensor_copy(out=whole[:], in_=for_sin)
         nc.vector.scalar_tensor_tensor(out=for_sin, in0=whole[:], scalar=-1.0, in1=for_sin, op0=ALU.mult, op1=ALU.add)
         nc.vector.scalar_tensor_tensor(out=for_sin, in0=for_sin, scalar=0.5, in1=for_sin, op0=ALU.is_gt, op1=ALU.subtract)
-        nc.scalar.activation(out=for_cos, in_=for_sin, func=ACT.Abs)
-        nc.scalar.activation(out=for_cos, in_=for_cos, func=ACT.Copy, scale=-1.0, bias=0.25)
         trig = keep.tile([P, 2, TILES, HALF], F32, name="trig")
-        for part, turn in ((0, 2.0 * math.pi), (1, -2.0 * math.pi)):
-            nc.scalar.activation(out=trig[:, part, :, :].rearrange("p i (a b) -> p i a b", b=8),
-                                 in_=angles[:, part, :, :].rearrange("p b (a i) -> p i a b", i=TILES),
-                                 func=ACT.Sin, scale=turn)
+
+        def sines():
+            nc.scalar.activation(out=for_cos, in_=for_sin, func=ACT.Abs)
+            nc.scalar.activation(out=for_cos, in_=for_cos, func=ACT.Copy, scale=-1.0, bias=0.25)
+            for part, turn in ((0, 2.0 * math.pi), (1, -2.0 * math.pi)):
+                nc.scalar.activation(out=trig[:, part, :, :].rearrange("p i (a b) -> p i a b", b=8),
+                                     in_=angles[:, part, :, :].rearrange("p b (a i) -> p i a b", i=TILES),
+                                     func=ACT.Sin, scale=turn)
 
         gain = keep.tile([P, 2, 3, HALF], F32, name="gain")
         tables = []
@@ -162,7 +165,7 @@ def tile_gemma3mhattention_pa_kernel(
         def build_gain(kind):
             s = HEAD ** -0.5 if kind == 0 else 1.0
             for n, (half, factor) in enumerate(((0, s), (1, -s), (1, s))):
-                nc.vector.tensor_scalar(out=gain[:, kind, n, :], in0=norm_w[:, kind, HALF * half : HALF * (half + 1)],
+                nc.gpsimd.tensor_scalar(out=gain[:, kind, n, :], in0=norm_w[:, kind, HALF * half : HALF * (half + 1)],
                                         scalar1=1.0, scalar2=factor, op0=ALU.add, op1=ALU.mult)
 
         build_gain(0)
@@ -193,10 +196,10 @@ def tile_gemma3mhattention_pa_kernel(
             w_blocks.append(w_blocks_c)
 
         built = []
-        x_wide, grouped, turned, sums, squares, inv_rms, products, results = {}, {}, {}, {}, {}, {}, {}, {}
+        x_wide, grouped, twins, turned, sums, squares, inv_rms, products, results = {}, {}, {}, {}, {}, {}, {}, {}, {}
 
         def widen(i):
-            wide = work.tile([P, FEATURES], BF16, name="wide", tag="wide", bufs=4)
+            wide = work.tile([P, FEATURES], BF16, name="wide", tag="wide", bufs=3)
             width = K_PASS if i == 0 else FEATURES
             for k0 in range(0, FEATURES, width):
                 nc.vector.tensor_tensor(out=wide[:, k0 : k0 + width], in0=x_codes_in[:, i, k0 : k0 + width].bitcast(FP8),
@@ -210,8 +213,14 @@ def tile_gemma3mhattention_pa_kernel(
 
         def transposes(units):
             for unit in units:
-                group_tile = work.tile([P, 4, P, 4], BF16, name="grouped", tag="grouped", bufs=4, align_bytes=64)
-                grouped[unit] = group_tile
+                if unit[0] == "x":
+                    group_tile = work.tile([P, 4, P, 4], BF16, name="grouped", tag="grouped", bufs=2, align_bytes=64)
+                    grouped[unit] = group_tile[:]
+                elif unit[2] % 2 == 0:
+                    twin_tile = work.tile([P, 2, 4, P, 4], BF16, name="twin", tag="twin", bufs=2, align_bytes=64)
+                    grouped[unit] = twin_tile[:, 0, :, :, :]
+                    grouped[(unit[0], unit[1], unit[2] + 1)] = twin_tile[:, 1, :, :, :]
+                    twins[(unit[1], unit[2] + 1)] = twin_tile
                 banks = []
                 for b in range(2):
                     bank = ps.tile([P, 2, 2, P], F32, name="turned", tag="bank")
@@ -225,18 +234,23 @@ def tile_gemma3mhattention_pa_kernel(
                             nc.tensor.transpose(turned[unit][b][:, a, u, :], words[:, u : WORDS : 2], ident[:])
 
         def copy_out(unit):
-            words = grouped[unit][:].rearrange("p n r t -> p (n r t)").bitcast(F32)
+            words = grouped[unit].rearrange("p n r t -> p (n r t)").bitcast(F32)
             words = words.rearrange("p (n r u) -> p n r u", n=4, u=2)
             for b in range(2):
                 nc.scalar.copy(out=words[:, 2 * b : 2 * b + 2, :, :],
                                in_=turned[unit][b][:].rearrange("p a u r -> p a r u"))
 
         def quantize(unit):
-            values = grouped[unit][:].rearrange("p n r t -> p (n r t)")
             if unit[0] == "x":
+                values = grouped[unit].rearrange("p n r t -> p (n r t)")
                 codes, blocks = x_codes[:, unit[1], :], x_blocks[:, unit[1], :]
             else:
-                codes, blocks = w_codes[unit[1]][:, unit[2], :], w_blocks[unit[1]][:, unit[2], :]
+                c, g = unit[1], unit[2]
+                if g % 2 == 0:
+                    return
+                values = twins[(c, g)][:].rearrange("p a n r t -> p (a n r t)")
+                codes = w_codes[c][:, g - 1 : g + 1, :].rearrange("p g n -> p (g n)")
+                blocks = w_blocks[c][:, g - 1 : g + 1, :].rearrange("p g n -> p (g n)")
             nc.vector.quantize_mx(out=codes.bitcast(FP8X4), scales=blocks, in_=values)
 
         def matmuls(t):
@@ -325,6 +339,8 @@ def tile_gemma3mhattention_pa_kernel(
                 store(t - COPY_LAG)
             for unit in units_at(t):
                 copy_out(unit)
+            if t == SINES_STEP:
+                sines()
             if units_at(t) and not units_at(t + 1):
                 nc.scalar.activation(out=warm[:], in_=zero[:], func=ACT.Abs_reciprocal_sqrt, bias=1.0)
             if is_rope(t - PRODUCTS_LAG):

@@ -34,7 +34,8 @@ PRODUCTS_LAG = 3
 ADD_LAG = 4
 WIDEN_LEAD = 5
 LOAD_LEAD = 6
-SINES_STEP = 12
+SINES_STEP = 11
+SINGLE_ADDS = 4
 V_LAST = 2
 
 
@@ -63,7 +64,6 @@ def tile_gemma3mhattention_pa_kernel(
         steps.append(([], (i, n_groups - 1)))
     n_steps = len(steps)
     rope_steps = [t for t in range(n_steps) if steps[t][1] is not None and groups[steps[t][1][1]][4] is not None]
-    n_pairs = len(rope_steps) // 2
 
     def units_at(t):
         return steps[t][0] if 0 <= t < n_steps else []
@@ -148,13 +148,20 @@ def tile_gemma3mhattention_pa_kernel(
         nc.vector.scalar_tensor_tensor(out=for_sin, in0=for_sin, scalar=0.5, in1=for_sin, op0=ALU.is_gt, op1=ALU.subtract)
         trig = keep.tile([P, 2, TILES, HALF], F32, name="trig")
 
-        def sines():
-            nc.scalar.activation(out=for_cos, in_=for_sin, func=ACT.Abs)
-            nc.scalar.activation(out=for_cos, in_=for_cos, func=ACT.Copy, scale=-1.0, bias=0.25)
-            for part, turn in ((0, 2.0 * math.pi), (1, -2.0 * math.pi)):
-                nc.scalar.activation(out=trig[:, part, :, :].rearrange("p i (a b) -> p i a b", b=8),
-                                     in_=angles[:, part, :, :].rearrange("p b (a i) -> p i a b", i=TILES),
-                                     func=ACT.Sin, scale=turn)
+        def sine(part, turn):
+            nc.scalar.activation(out=trig[:, part, :, :].rearrange("p i (a b) -> p i a b", b=8),
+                                 in_=angles[:, part, :, :].rearrange("p b (a i) -> p i a b", i=TILES),
+                                 func=ACT.Sin, scale=turn)
+
+        def sines(n):
+            if n == 0:
+                nc.scalar.activation(out=for_cos, in_=for_sin, func=ACT.Abs)
+            elif n == 1:
+                nc.scalar.activation(out=for_cos, in_=for_cos, func=ACT.Copy, scale=-1.0, bias=0.25)
+            elif n == 2:
+                sine(1, -2.0 * math.pi)
+            elif n == 3:
+                sine(0, 2.0 * math.pi)
 
         gain = keep.tile([P, 2, 3, HALF], F32, name="gain")
         tables = []
@@ -196,10 +203,10 @@ def tile_gemma3mhattention_pa_kernel(
             w_blocks.append(w_blocks_c)
 
         built = []
-        x_wide, grouped, twins, turned, sums, squares, inv_rms, products, results = {}, {}, {}, {}, {}, {}, {}, {}, {}
+        x_wide, grouped, twins, turned, sums, squares, inv_rms, products, pair_results, results = {}, {}, {}, {}, {}, {}, {}, {}, {}, {}
 
         def widen(i):
-            wide = work.tile([P, FEATURES], BF16, name="wide", tag="wide", bufs=3)
+            wide = work.tile([P, FEATURES], BF16, name="wide", tag="four_kib", bufs=4)
             width = K_PASS if i == 0 else FEATURES
             for k0 in range(0, FEATURES, width):
                 nc.vector.tensor_tensor(out=wide[:, k0 : k0 + width], in0=x_codes_in[:, i, k0 : k0 + width].bitcast(FP8),
@@ -213,14 +220,12 @@ def tile_gemma3mhattention_pa_kernel(
 
         def transposes(units):
             for unit in units:
-                if unit[0] == "x":
-                    group_tile = work.tile([P, 4, P, 4], BF16, name="grouped", tag="grouped", bufs=2, align_bytes=64)
-                    grouped[unit] = group_tile[:]
-                elif unit[2] % 2 == 0:
-                    twin_tile = work.tile([P, 2, 4, P, 4], BF16, name="twin", tag="twin", bufs=2, align_bytes=64)
+                if unit[-1] % 2 == 0:
+                    twin_tile = work.tile([P, 2, 4, P, 4], BF16, name="twin", tag="twin", bufs=4, align_bytes=64)
+                    second = unit[:-1] + (unit[-1] + 1,)
                     grouped[unit] = twin_tile[:, 0, :, :, :]
-                    grouped[(unit[0], unit[1], unit[2] + 1)] = twin_tile[:, 1, :, :, :]
-                    twins[(unit[1], unit[2] + 1)] = twin_tile
+                    grouped[second] = twin_tile[:, 1, :, :, :]
+                    twins[second] = twin_tile
                 banks = []
                 for b in range(2):
                     bank = ps.tile([P, 2, 2, P], F32, name="turned", tag="bank")
@@ -241,17 +246,13 @@ def tile_gemma3mhattention_pa_kernel(
                                in_=turned[unit][b][:].rearrange("p a u r -> p a r u"))
 
         def quantize(unit):
-            if unit[0] == "x":
-                values = grouped[unit].rearrange("p n r t -> p (n r t)")
-                codes, blocks = x_codes[:, unit[1], :], x_blocks[:, unit[1], :]
-            else:
-                c, g = unit[1], unit[2]
-                if g % 2 == 0:
-                    return
-                values = twins[(c, g)][:].rearrange("p a n r t -> p (a n r t)")
-                codes = w_codes[c][:, g - 1 : g + 1, :].rearrange("p g n -> p (g n)")
-                blocks = w_blocks[c][:, g - 1 : g + 1, :].rearrange("p g n -> p (g n)")
-            nc.vector.quantize_mx(out=codes.bitcast(FP8X4), scales=blocks, in_=values)
+            if unit not in twins:
+                return
+            n = unit[-1]
+            codes, blocks = (x_codes, x_blocks) if unit[0] == "x" else (w_codes[unit[1]], w_blocks[unit[1]])
+            nc.vector.quantize_mx(out=codes[:, n - 1 : n + 1, :].rearrange("p a n -> p (a n)").bitcast(FP8X4),
+                                  scales=blocks[:, n - 1 : n + 1, :].rearrange("p a n -> p (a n)"),
+                                  in_=twins[unit][:].rearrange("p a n r t -> p (a n r t)"))
 
         def matmuls(t):
             i, c = bank_at(t)
@@ -300,24 +301,25 @@ def tile_gemma3mhattention_pa_kernel(
                     op1=ALU.mult,
                 )
 
-        def add_halves(n):
-            result = work.tile([P, 2, HEADS, HEAD], F32, name="result", tag="result", bufs=4)
-            shares = products[n][:].rearrange("p b h t s d -> p (b h t) s d")
-            engine = nc.vector if n >= n_pairs - 2 else nc.gpsimd
-            engine.tensor_tensor(out=result[:].rearrange("p b h (t d) -> p (b h t) d", t=2), in0=shares[:, :, 0, :],
-                                 in1=shares[:, :, 1, :], op=ALU.add)
-            for b in range(2):
-                results[rope_steps[2 * n + b]] = result[:, b, :, :]
+        def add_halves(engine, n, b0, b1):
+            if n not in pair_results:
+                result = work.tile([P, 2, HEADS, HEAD], F32, name="result", tag="four_kib", bufs=4)
+                pair_results[n] = result
+            shares = products[n][:, b0:b1, :, :, :, :].rearrange("p b h t s d -> p (b h t) s d")
+            engine.tensor_tensor(out=pair_results[n][:, b0:b1, :, :].rearrange("p b h (t d) -> p (b h t) d", t=2),
+                                 in0=shares[:, :, 0, :], in1=shares[:, :, 1, :], op=ALU.add)
+            for b in range(b0, b1):
+                results[rope_steps[2 * n + b]] = pair_results[n][:, b, :, :]
 
         def copy_plain(t):
             plain = work.tile([P, HEADS, HEAD], F32, name="plain", tag="plain", bufs=3)
             nc.scalar.copy(out=plain[:].rearrange("p h e -> p (h e)"), in_=sums[t][:])
             results[t] = plain
 
-        def store(t):
+        def store(t, queue):
             i, c = bank_at(t)
             dst, h0 = groups[c][2], groups[c][3]
-            nc.sync.dma_start(
+            queue.dma_start(
                 out=dst[0, h0 : h0 + HEADS, P * i : P * (i + 1), :].rearrange("h p d -> p h d"),
                 in_=results[t][:],
             )
@@ -336,11 +338,10 @@ def tile_gemma3mhattention_pa_kernel(
                 inverse_rms(t - SQUARES_LAG)
             if is_plain(t - COPY_LAG):
                 copy_plain(t - COPY_LAG)
-                store(t - COPY_LAG)
+                store(t - COPY_LAG, nc.scalar if t - COPY_LAG >= n_steps - V_LAST else nc.sync)
             for unit in units_at(t):
                 copy_out(unit)
-            if t == SINES_STEP:
-                sines()
+            sines(t - SINES_STEP)
             if units_at(t) and not units_at(t + 1):
                 nc.scalar.activation(out=warm[:], in_=zero[:], func=ACT.Abs_reciprocal_sqrt, bias=1.0)
             if is_rope(t - PRODUCTS_LAG):
@@ -350,8 +351,12 @@ def tile_gemma3mhattention_pa_kernel(
                     widen(unit[1])
             for unit in units_at(t - 1):
                 quantize(unit)
-            if is_rope(t - ADD_LAG) and rope_steps.index(t - ADD_LAG) % 2 == 1:
-                pair = rope_steps.index(t - ADD_LAG) // 2
-                add_halves(pair)
-                store(rope_steps[2 * pair])
-                store(rope_steps[2 * pair + 1])
+            if is_rope(t - ADD_LAG):
+                r = rope_steps.index(t - ADD_LAG)
+                if r >= len(rope_steps) - SINGLE_ADDS:
+                    add_halves(nc.gpsimd if r < len(rope_steps) - SINGLE_ADDS // 2 else nc.vector, r // 2, r % 2, r % 2 + 1)
+                    store(rope_steps[r], nc.sync)
+                elif r % 2 == 1:
+                    add_halves(nc.gpsimd, r // 2, 0, 2)
+                    store(rope_steps[r - 1], nc.sync)
+                    store(rope_steps[r], nc.sync)

@@ -36,7 +36,7 @@ WIDEN_LEAD = 5
 LOAD_LEAD = 6
 SINES_STEP = 11
 SINGLE_ADDS = 4
-V_LAST = 2
+V_LAST = 1
 
 
 def tile_gemma3mhattention_pa_kernel(
@@ -338,7 +338,7 @@ def tile_gemma3mhattention_pa_kernel(
                 inverse_rms(t - SQUARES_LAG)
             if is_plain(t - COPY_LAG):
                 copy_plain(t - COPY_LAG)
-                store(t - COPY_LAG, nc.scalar if t - COPY_LAG >= n_steps - V_LAST else nc.sync)
+                store(t - COPY_LAG, nc.scalar)
             for unit in units_at(t):
                 copy_out(unit)
             sines(t - SINES_STEP)

@@ -35,7 +35,8 @@ ADD_LAG = 4
 WIDEN_LEAD = 5
 LOAD_LEAD = 6
 SINES_STEP = 11
-SINGLE_ADDS = 4
+SINGLE_ADDS = 8
+VECTOR_ADDS = 2
 V_LAST = 1
 
 
@@ -354,7 +355,7 @@ def tile_gemma3mhattention_pa_kernel(
             if is_rope(t - ADD_LAG):
                 r = rope_steps.index(t - ADD_LAG)
                 if r >= len(rope_steps) - SINGLE_ADDS:
-                    add_halves(nc.gpsimd if r < len(rope_steps) - SINGLE_ADDS // 2 else nc.vector, r // 2, r % 2, r % 2 + 1)
+                    add_halves(nc.gpsimd if r < len(rope_steps) - VECTOR_ADDS else nc.vector, r // 2, r % 2, r % 2 + 1)
                     store(rope_steps[r], nc.sync)
                 elif r % 2 == 1:
                     add_halves(nc.gpsimd, r // 2, 0, 2)

@@ -84,8 +84,8 @@ def tile_gemma3mhattention_pa_kernel(
         ps = ctx.enter_context(tc.psum_pool(name="ps", bufs=8))
         ctx.enter_context(tc.manual_schedule())
 
-        scale_cols = keep.tile([P, PASSES, 4], F32, name="scale_cols")
-        nc.sync.dma_start(out=scale_cols[:], in_=x_scale.rearrange("a b (g q t) -> (a b q) g t", g=PASSES, t=4))
+        scale_cols = keep.tile([P, 2, 8], F32, name="scale_cols")
+        nc.sync.dma_start(out=scale_cols[:], in_=x_scale.rearrange("a b (g q t) -> (a b q) g t", g=2, t=8))
         scales = keep.tile([P, FEATURES], F32, name="scales")
         norm_w = keep.tile([P, 2, HEAD], BF16, name="norm_w")
 
@@ -126,12 +126,13 @@ def tile_gemma3mhattention_pa_kernel(
         ident = keep.tile([P, P], F32, name="ident")
         make_identity(nc, ident[:])
 
-        for g in range(PASSES):
-            spread = ps.tile([P, 4, P], F32, name="spread", tag="bank")
-            for n in range(4):
-                nc.tensor.transpose(spread[:, n, :], scale_cols[:, g, n : n + 1].to_broadcast([P, P]), ident[:])
-            nc.scalar.copy(out=scales[:, K_PASS * g : K_PASS * (g + 1)].rearrange("p (q t) -> p q t", t=4),
-                           in_=spread[:].rearrange("p t q -> p q t"))
+        for a in range(2):
+            for h in range(2):
+                spread = ps.tile([P, 4, P], F32, name="spread", tag="bank")
+                for n in range(4):
+                    nc.tensor.transpose(spread[:, n, :], scale_cols[:, a, 4 * h + n : 4 * h + n + 1].to_broadcast([P, P]), ident[:])
+                half = scales[:, FEATURES // 2 * a : FEATURES // 2 * (a + 1)].rearrange("p (q h t) -> p q h t", h=2, t=4)
+                nc.scalar.copy(out=half[:, :, h, :], in_=spread[:].rearrange("p t q -> p q t"))
 
         coarse = keep.tile([P, 8, TILES], F32, name="coarse")
         for a in range(8):
@@ -208,7 +209,7 @@ def tile_gemma3mhattention_pa_kernel(
 
         def widen(i):
             wide = work.tile([P, FEATURES], BF16, name="wide", tag="four_kib", bufs=4)
-            width = K_PASS if i == 0 else FEATURES
+            width = FEATURES // 2 if i == 0 else FEATURES
             for k0 in range(0, FEATURES, width):
                 nc.vector.tensor_tensor(out=wide[:, k0 : k0 + width], in0=x_codes_in[:, i, k0 : k0 + width].bitcast(FP8),
                                         in1=scales[:, k0 : k0 + width], op=ALU.mult)

from contextlib import ExitStack
import math

import concourse.mybir as mybir
from concourse.masks import make_identity

TOKENS, FEATURES, HEAD = 1024, 2048, 128
EPS = 1e-6
THETA = 10000.0
FLOPS = 2 * TOKENS * FEATURES * 2048

F32 = mybir.dt.float32
BF16 = mybir.dt.bfloat16
U32 = mybir.dt.uint32
U8 = mybir.dt.uint8
I32 = mybir.dt.int32
FP8 = mybir.dt.float8_e4m3fn
FP8X4 = mybir.dt.float8_e4m3fn_x4
ALU = mybir.AluOpType
ACT = mybir.ActivationFunctionType

P = 128
K_PASS = 512
PASSES = FEATURES // K_PASS
TILES = TOKENS // P
GROUP = 512
HEADS = GROUP // HEAD
HALF = HEAD // 2
WORDS = K_PASS // 2

SQUARES_LAG = 1
COPY_LAG = 2
PRODUCTS_LAG = 3
ADD_LAG = 4
WIDEN_LEAD = 5
LOAD_LEAD = 6
SINES_STEP = 11
SINGLE_ADDS = 8
VECTOR_ADDS = 2
V_LAST = 1


def tile_gemma3mhattention_pa_kernel(
    tc, x_bytes, x_scale, wq, wk, wv, q_norm_w, k_norm_w, out_0, out_1, out_2
):
    nc = tc.nc
    groups = [
        (wq, 0, out_0, 0, 0),
        (wq, GROUP, out_0, HEADS, 0),
        (wk, 0, out_1, 0, 1),
        (wv, 0, out_2, 0, None),
    ]
    n_groups = len(groups)

    steps = []
    for n in range(TILES):
        for m in (2 * n, 2 * n + 1):
            steps.append(([("w", m // PASSES, m % PASSES)], None))
        steps.append(([("x", n)], None))
    for i in range(TILES):
        for c in range(n_groups):
            if groups[c][4] is not None or i < TILES - V_LAST:
                steps.append(([], (i, c)))
    for i in range(TILES - V_LAST, TILES):
        steps.append(([], (i, n_groups - 1)))
    n_steps = len(steps)
    rope_steps = [t for t in range(n_steps) if steps[t][1] is not None and groups[steps[t][1][1]][4] is not None]

    def units_at(t):
        return steps[t][0] if 0 <= t < n_steps else []

    def bank_at(t):
        return steps[t][1] if 0 <= t < n_steps else None

    def is_rope(t):
        return t in rope_steps

    def is_plain(t):
        return bank_at(t) is not None and not is_rope(t)

    with ExitStack() as ctx:
        keep = ctx.enter_context(tc.tile_pool(name="keep", bufs=1))
        work = ctx.enter_context(tc.tile_pool(name="work", bufs=2))
        ps = ctx.enter_context(tc.psum_pool(name="ps", bufs=8))
        ctx.enter_context(tc.manual_schedule())

        scale_cols = keep.tile([P, 2, 8], F32, name="scale_cols")
        nc.sync.dma_start(out=scale_cols[:], in_=x_scale.rearrange("a b (g q t) -> (a b q) g t", g=2, t=8))
        scales = keep.tile([P, FEATURES], F32, name="scales")
        norm_w = keep.tile([P, 2, HEAD], BF16, name="norm_w")

        x_rows = x_bytes.rearrange("o (i p) k -> p (o i) k", p=P)
        x_codes_in = keep.tile([P, TILES, FEATURES], U8, name="x_codes_in")
        w_raw = []
        for c in range(n_groups):
            w_raw_c = work.tile([P, PASSES, HEADS, K_PASS], BF16, name="w_raw%d" % c, tag="big", bufs=4)
            w_raw.append(w_raw_c)

        def load_w_pass(c, g):
            w, r0 = groups[c][0], groups[c][1]
            nc.sync.dma_start(
                out=w_raw[c][:, g, :, :],
                in_=w[r0 : r0 + GROUP, K_PASS * g : K_PASS * (g + 1)].rearrange("(r p) k -> p r k", p=P),
            )

        def load_x(i0, i1):
            nc.sync.dma_start(out=x_codes_in[:, i0:i1, :], in_=x_rows[:, i0:i1, :])

        for t in range(-LOAD_LEAD, n_steps):
            for unit in units_at(t):
                if unit[0] == "w":
                    load_w_pass(unit[1], unit[2])
            for unit in units_at(t + LOAD_LEAD):
                if unit[0] == "x":
                    load_x(unit[1], unit[1] + 1)
        nc.sync.dma_start(out=norm_w[:, 0, :], in_=q_norm_w.partition_broadcast(P))
        nc.sync.dma_start(out=norm_w[:, 1, :], in_=k_norm_w.partition_broadcast(P))

        position = keep.tile([P, TILES], F32, name="position")
        nc.gpsimd.iota(position[:], pattern=[[P, TILES]], base=0, channel_multiplier=1,
                       allow_small_or_imprecise_dtypes=True)
        zero = keep.tile([P, 1], F32, name="zero")
        nc.gpsimd.memset(zero[:], 0.0)
        warm = keep.tile([P, 1], F32, name="warm")
        nc.scalar.activation(out=warm[:], in_=zero[:], func=ACT.Sin)
        ident = keep.tile([P, P], F32, name="ident")
        make_identity(nc, ident[:])

        for a in range(2):
            for h in range(2):
                spread = ps.tile([P, 4, P], F32, name="spread", tag="bank")
                for n in range(4):
                    nc.tensor.transpose(spread[:, n, :], scale_cols[:, a, 4 * h + n : 4 * h + n + 1].to_broadcast([P, P]), ident[:])
                half = scales[:, FEATURES // 2 * a : FEATURES // 2 * (a + 1)].rearrange("p (q h t) -> p q h t", h=2, t=4)
                nc.scalar.copy(out=half[:, :, h, :], in_=spread[:].rearrange("p t q -> p q t"))

        coarse = keep.tile([P, 8, TILES], F32, name="coarse")
        for a in range(8):
            nc.vector.tensor_scalar_mul(out=coarse[:, a, :], in0=position[:],
                                        scalar1=THETA ** (-8.0 * a / HALF) / (2.0 * math.pi))
        angles = keep.tile([P, 2, 8, 8 * TILES], F32, name="angles")
        for b in range(8):
            nc.vector.tensor_scalar_mul(out=angles[:, 1, b, :], in0=coarse[:].rearrange("p a i -> p (a i)"),
                                        scalar1=THETA ** (-1.0 * b / HALF))
        for_cos = angles[:, 0, :, :].rearrange("p b n -> p (b n)")
        for_sin = angles[:, 1, :, :].rearrange("p b n -> p (b n)")
        whole = keep.tile([P, TILES * HALF], I32, name="whole")
        nc.vector.tensor_copy(out=whole[:], in_=for_sin)
        nc.vector.scalar_tensor_tensor(out=for_sin, in0=whole[:], scalar=-1.0, in1=for_sin, op0=ALU.mult, op1=ALU.add)
        nc.vector.scalar_tensor_tensor(out=for_sin, in0=for_sin, scalar=0.5, in1=for_sin, op0=ALU.is_gt, op1=ALU.subtract)
        trig = keep.tile([P, 2, TILES, HALF], F32, name="trig")

        def sine(part, turn):
            nc.scalar.activation(out=trig[:, part, :, :].rearrange("p i (a b) -> p i a b", b=8),
                                 in_=angles[:, part, :, :].rearrange("p b (a i) -> p i a b", i=TILES),
                                 func=ACT.Sin, scale=turn)

        def sines(n):
            if n == 0:
                nc.scalar.activation(out=for_cos, in_=for_sin, func=ACT.Abs)
            elif n == 1:
                nc.scalar.activation(out=for_cos, in_=for_cos, func=ACT.Copy, scale=-1.0, bias=0.25)
            elif n == 2:
                sine(1, -2.0 * math.pi)
            elif n == 3:
                sine(0, 2.0 * math.pi)

        gain = keep.tile([P, 2, 3, HALF], F32, name="gain")
        tables = []
        for kind in range(2):
            table = keep.tile([P, TILES, 2, 2, HALF], F32, name="table%d" % kind)
            tables.append(table)

        def build_gain(kind):
            s = HEAD ** -0.5 if kind == 0 else 1.0
            for n, (half, factor) in enumerate(((0, s), (1, -s), (1, s))):
                nc.gpsimd.tensor_scalar(out=gain[:, kind, n, :], in0=norm_w[:, kind, HALF * half : HALF * (half + 1)],
                                        scalar1=1.0, scalar2=factor, op0=ALU.add, op1=ALU.mult)

        build_gain(0)
        build_gain(1)

        def build_table(kind):
            nc.vector.tensor_tensor(
                out=tables[kind][:, :, :, 0, :],
                in0=trig[:].rearrange("p c i d -> p i c d"),
                in1=gain[:, kind, 0, :].unsqueeze(1).unsqueeze(1).to_broadcast([P, TILES, 2, HALF]),
                op=ALU.mult,
            )
            for dst in range(2):
                nc.vector.tensor_tensor(
                    out=tables[kind][:, :, dst, 1, :],
                    in0=trig[:, 1 - dst, :, :],
                    in1=gain[:, kind, 1 + dst, :].unsqueeze(1).to_broadcast([P, TILES, HALF]),
                    op=ALU.mult,
                )

        x_codes = keep.tile([P, TILES, PASSES * P], U32, name="x_codes", align_bytes=256)
        x_blocks = keep.tile([P, TILES, PASSES * P], U8, name="x_blocks", align_bytes=256)
        w_codes, w_blocks = [], []
        for c in range(n_groups):
            w_codes_c = keep.tile([P, PASSES, GROUP], U32, name="w_codes%d" % c, align_bytes=256)
            w_blocks_c = keep.tile([P, PASSES, GROUP], U8, name="w_blocks%d" % c, align_bytes=256)
            w_codes.append(w_codes_c)
            w_blocks.append(w_blocks_c)

        built = []
        x_wide, grouped, twins, turned, sums, squares, inv_rms, products, pair_results, results = {}, {}, {}, {}, {}, {}, {}, {}, {}, {}

        def widen(i):
            wide = work.tile([P, FEATURES], BF16, name="wide", tag="four_kib", bufs=4)
            width = FEATURES // 2 if i == 0 else FEATURES
            for k0 in range(0, FEATURES, width):
                nc.vector.tensor_tensor(out=wide[:, k0 : k0 + width], in0=x_codes_in[:, i, k0 : k0 + width].bitcast(FP8),
                                        in1=scales[:, k0 : k0 + width], op=ALU.mult)
            x_wide[i] = wide

        def rows_and_pass(unit, n):
            if unit[0] == "x":
                return x_wide[unit[1]][:, K_PASS * n : K_PASS * (n + 1)].bitcast(F32)
            return w_raw[unit[1]][:, unit[2], n, :].bitcast(F32)

        def transposes(units):
            for unit in units:
                if unit[-1] % 2 == 0:
                    twin_tile = work.tile([P, 2, 4, P, 4], BF16, name="twin", tag="twin", bufs=4, align_bytes=64)
                    second = unit[:-1] + (unit[-1] + 1,)
                    grouped[unit] = twin_tile[:, 0, :, :, :]
                    grouped[second] = twin_tile[:, 1, :, :, :]
                    twins[second] = twin_tile
                banks = []
                for b in range(2):
                    bank = ps.tile([P, 2, 2, P], F32, name="turned", tag="bank")
                    banks.append(bank)
                turned[unit] = banks
            for unit in units:
                for a in range(2):
                    for u in range(2):
                        for b in range(2):
                            words = rows_and_pass(unit, 2 * b + a)
                            nc.tensor.transpose(turned[unit][b][:, a, u, :], words[:, u : WORDS : 2], ident[:])

        def copy_out(unit):
            words = grouped[unit].rearrange("p n r t -> p (n r t)").bitcast(F32)
            words = words.rearrange("p (n r u) -> p n r u", n=4, u=2)
            for b in range(2):
                nc.scalar.copy(out=words[:, 2 * b : 2 * b + 2, :, :],
                               in_=turned[unit][b][:].rearrange("p a u r -> p a r u"))

        def quantize(unit):
            if unit not in twins:
                return
            n = unit[-1]
            codes, blocks = (x_codes, x_blocks) if unit[0] == "x" else (w_codes[unit[1]], w_blocks[unit[1]])
            nc.vector.quantize_mx(out=codes[:, n - 1 : n + 1, :].rearrange("p a n -> p (a n)").bitcast(FP8X4),
                                  scales=blocks[:, n - 1 : n + 1, :].rearrange("p a n -> p (a n)"),
                                  in_=twins[unit][:].rearrange("p a n r t -> p (a n r t)"))

        def matmuls(t):
            i, c = bank_at(t)
            acc = ps.tile([P, GROUP], F32, name="acc", tag="bank")
            for g in range(PASSES):
                nc.tensor.matmul_mx(
                    out=acc[:],
                    lhsT=x_codes[:, i, P * g : P * (g + 1)].bitcast(FP8X4),
                    lhsT_scale=x_blocks[:, i, P * g : P * (g + 1)],
                    rhs=w_codes[c][:, g, :].bitcast(FP8X4),
                    rhs_scale=w_blocks[c][:, g, :],
                    start=(g == 0),
                    stop=(g == PASSES - 1),
                )
            sums[t] = acc

        def sum_squares(t):
            total = work.tile([P, HEADS], F32, name="total", tag="total", bufs=6)
            unused = work.tile([P, HEADS, HEAD], BF16, name="unused", tag="unused", bufs=2)
            for h in range(HEADS):
                nc.scalar.activation(out=unused[:, h, :], in_=sums[t][:, HEAD * h : HEAD * (h + 1)], func=ACT.Square,
                                     accum_out=total[:, h : h + 1])
            squares[t] = total

        def inverse_rms(t):
            inv = work.tile([P, HEADS], F32, name="inv", tag="inv", bufs=6)
            nc.scalar.activation(out=inv[:], in_=squares[t][:], func=ACT.Abs_reciprocal_sqrt, scale=1.0 / HEAD, bias=EPS)
            inv_rms[t] = inv

        def table_products(t):
            i, c = bank_at(t)
            r = rope_steps.index(t)
            if groups[c][4] not in built:
                build_table(groups[c][4])
                built.append(groups[c][4])
            if r % 2 == 0:
                pair_tile = work.tile([P, 2, HEADS, 2, 2, HALF], F32, name="pair", tag="big", bufs=4)
                products[r // 2] = pair_tile
            for h in range(HEADS):
                nc.vector.scalar_tensor_tensor(
                    out=products[r // 2][:, r % 2, h, :, :, :].rearrange("p t s d -> p t (s d)"),
                    in0=sums[t][:, HEAD * h : HEAD * (h + 1)].unsqueeze(1).to_broadcast([P, 2, HEAD]),
                    scalar=inv_rms[t][:, h : h + 1],
                    in1=tables[groups[c][4]][:, i, :, :, :].rearrange("p t s d -> p t (s d)"),
                    op0=ALU.mult,
                    op1=ALU.mult,
                )

        def add_halves(engine, n, b0, b1):
            if n not in pair_results:
                result = work.tile([P, 2, HEADS, HEAD], F32, name="result", tag="four_kib", bufs=4)
                pair_results[n] = result
            shares = products[n][:, b0:b1, :, :, :, :].rearrange("p b h t s d -> p (b h t) s d")
            engine.tensor_tensor(out=pair_results[n][:, b0:b1, :, :].rearrange("p b h (t d) -> p (b h t) d", t=2),
                                 in0=shares[:, :, 0, :], in1=shares[:, :, 1, :], op=ALU.add)
            for b in range(b0, b1):
                results[rope_steps[2 * n + b]] = pair_results[n][:, b, :, :]

        def copy_plain(t):
            plain = work.tile([P, HEADS, HEAD], F32, name="plain", tag="plain", bufs=3)
            nc.scalar.copy(out=plain[:].rearrange("p h e -> p (h e)"), in_=sums[t][:])
            results[t] = plain

        def store(t, queue):
            i, c = bank_at(t)
            dst, h0 = groups[c][2], groups[c][3]
            queue.dma_start(
                out=dst[0, h0 : h0 + HEADS, P * i : P * (i + 1), :].rearrange("h p d -> p h d"),
                in_=results[t][:],
            )

        for t in range(WIDEN_LEAD):
            for unit in units_at(t):
                if unit[0] == "x":
                    widen(unit[1])
        for t in range(n_steps + ADD_LAG + 1):
            if units_at(t):
                transposes(units_at(t))
            if bank_at(t) is not None:
                matmuls(t)
            if is_rope(t - SQUARES_LAG):
                sum_squares(t - SQUARES_LAG)
                inverse_rms(t - SQUARES_LAG)
            if is_plain(t - COPY_LAG):
                copy_plain(t - COPY_LAG)
                store(t - COPY_LAG, nc.scalar)
            for unit in units_at(t):
                copy_out(unit)
            sines(t - SINES_STEP)
            if units_at(t) and not units_at(t + 1):
                nc.scalar.activation(out=warm[:], in_=zero[:], func=ACT.Abs_reciprocal_sqrt, bias=1.0)
            if is_rope(t - PRODUCTS_LAG):
                table_products(t - PRODUCTS_LAG)
            for unit in units_at(t + WIDEN_LEAD):
                if unit[0] == "x" and unit[1] not in x_wide:
                    widen(unit[1])
            for unit in units_at(t - 1):
                quantize(unit)
            if is_rope(t - ADD_LAG):
                r = rope_steps.index(t - ADD_LAG)
                if r >= len(rope_steps) - SINGLE_ADDS:
                    add_halves(nc.gpsimd if r < len(rope_steps) - VECTOR_ADDS else nc.vector, r // 2, r % 2, r % 2 + 1)
                    store(rope_steps[r], nc.sync)
                elif r % 2 == 1:
                    add_halves(nc.gpsimd, r // 2, 0, 2)
                    store(rope_steps[r - 1], nc.sync)
                    store(rope_steps[r], nc.sync)
